import numpy as np
import ml_dtypes

BF16 = ml_dtypes.bfloat16


def bf(x):
    return np.asarray(x, np.float32).astype(BF16)


def f32(x):
    return np.asarray(x, np.float32)


def f64(x):
    return np.asarray(x).astype(np.float64)


def striped(idx):
    return np.tile(idx.reshape(-1, 16).T, (8, 1))


V, E, S, N = 16, 256, 512, 128
EPS = 1e-5


def setup_inputs():
    return {"base": f32(np.random.standard_normal((E, S))), "edge": bf(np.random.standard_normal((E, N))), "x": bf(np.random.standard_normal((V, N))), "w": bf(np.random.standard_normal((N, N)) * np.sqrt(2.0 / N)), "gain": f32(1.0 + 0.1 * np.random.standard_normal((E, 1))), "bias": f32(0.1 * np.random.standard_normal((E, 1))), "offs": striped(np.random.permutation(S)[:N])}


def reference(base, edge, x, w, gain, bias, offs):
    idx = offs[:16].T.reshape(-1)
    e = f64(edge)
    m = e @ f64(w) + np.repeat(f64(x), V, axis=0) + np.tile(f64(x), (V, 1))
    mean = m.mean(axis=1, keepdims=True)
    var = ((m - mean) ** 2).mean(axis=1, keepdims=True)
    h = np.maximum((m - mean) / np.sqrt(var + EPS) * f64(gain) + f64(bias), 0.0)
    out = f64(base).copy()
    out[:, idx] = e + h
    return out

@@ -1,0 +1,89 @@
+import concourse.mybir as mybir
+from concourse.masks import make_identity
+
+P = 128
+EPS = 1e-5
+FLOPS = 2 * 256 * 128 * 128
+
+BF16, F32, U16 = mybir.dt.bfloat16, mybir.dt.float32, mybir.dt.uint16
+ALU = mybir.AluOpType
+ACT = mybir.ActivationFunctionType
+
+
+def tile_gnn_s2_kernel(tc, base, edge, x, w, gain, bias, offs, out):
+    nc = tc.nc
+    n_edges, n_slots = base.shape
+    n_nodes, n_feat = x.shape
+    assert n_edges == n_nodes * n_nodes and n_edges % P == 0 and n_feat == P
+    n_blocks = n_edges // P
+
+    base_blocks = base.rearrange("(b p) s -> b p s", p=P)
+    out_blocks = out.rearrange("(b p) s -> b p s", p=P)
+
+    with (
+        tc.tile_pool(name="held", bufs=1) as held,
+        tc.tile_pool(name="work", bufs=2) as work,
+        tc.psum_pool(name="psum", bufs=2) as psum,
+    ):
+        edge_sb = held.tile([P, n_blocks, n_feat], BF16, name="edge_sb")
+        nc.sync.dma_start(edge_sb[:], edge.rearrange("(b p) k -> p b k", p=P))
+        w_sb = held.tile([n_feat, n_feat], BF16, name="w_sb")
+        nc.scalar.dma_start(w_sb[:], w)
+        x_sb = held.tile([n_nodes, n_feat], BF16, name="x_sb")
+        nc.scalar.dma_start(x_sb[:], x)
+        offsets = held.tile([P, offs.shape[1]], U16, name="offsets")
+        nc.sync.dma_start(offsets[:], offs)
+        gain_sb = held.tile([P, n_blocks], F32, name="gain_sb")
+        bias_sb = held.tile([P, n_blocks], F32, name="bias_sb")
+        with nc.allow_non_contiguous_dma(reason="256 single values, one to a partition"):
+            nc.sync.dma_start(gain_sb[:], gain.rearrange("(b p) one -> p (b one)", p=P))
+            nc.scalar.dma_start(bias_sb[:], bias.rearrange("(b p) one -> p (b one)", p=P))
+        windows = [held.tile([P, n_slots], F32, name=f"window{b}") for b in range(n_blocks)]
+        nc.sync.dma_start(windows[0][:], base_blocks[0])
+        nc.scalar.dma_start(windows[1][:], base_blocks[1])
+
+        ident = held.tile([P, P], BF16, name="ident")
+        make_identity(nc, ident[:])
+        pick = held.tile([n_nodes, n_edges], BF16, name="pick")
+        small_ident = ident[0:n_nodes, 0:n_nodes]
+        cube = [n_nodes, n_nodes, n_nodes]
+        nc.vector.tensor_tensor(
+            pick[:].rearrange("v (a b) -> v a b", a=n_nodes),
+            small_ident.unsqueeze(2).to_broadcast(cube),
+            small_ident.unsqueeze(1).to_broadcast(cube),
+            ALU.add,
+        )
+
+        for b in range(n_blocks):
+            block = slice(b * P, (b + 1) * P)
+
+            edge_t_ps = psum.tile([n_feat, P], BF16, name="edge_t_ps")
+            nc.tensor.transpose(edge_t_ps[:], edge_sb[:, b, :], ident[:])
+            edge_t = work.tile([n_feat, P], BF16, name="edge_t")
+            nc.vector.tensor_copy(edge_t[:], edge_t_ps[:])
+
+            m_ps = psum.tile([P, n_feat], F32, name="m_ps")
+            nc.tensor.matmul(m_ps[:], pick[:, block], x_sb[:], start=True, stop=False)
+            nc.tensor.matmul(m_ps[:], edge_t[:], w_sb[:], start=False, stop=True)
+
+            stats = work.tile([P, 6], F32, name="stats")
+            nc.vector.bn_stats(stats[:], m_ps[:])
+            mean_var = work.tile([P, 2], F32, name="mean_var")
+            nc.vector.bn_aggr(mean_var[:], stats[:])
+            rstd = work.tile([P, 1], F32, name="rstd")
+            nc.scalar.activation(rstd[:], mean_var[:, 1:2], ACT.Sqrt, bias=EPS)
+            nc.vector.reciprocal(rstd[:], rstd[:])
+
+            normed = work.tile([P, n_feat], F32, name="normed")
+            nc.vector.tensor_scalar(
+                normed[:], m_ps[:], mean_var[:, 0:1], rstd[:], ALU.subtract, ALU.mult
+            )
+            h = work.tile([P, n_feat], F32, name="h")
+            nc.scalar.activation(
+                h[:], normed[:], ACT.Relu, bias=bias_sb[:, b : b + 1], scale=gain_sb[:, b : b + 1]
+            )
+
+            edge_f32 = work.tile([P, n_feat], F32, name="edge_f32")
+            nc.scalar.copy(edge_f32[:], edge_sb[:, b, :])
+            nc.vector.tensor_tensor(windows[b][:].indirect(offsets[:]), h[:], edge_f32[:], ALU.add)
+            nc.sync.dma_start(out_blocks[b], windows[b][:])

@@ -42,6 +42,10 @@ def tile_gnn_s2_kernel(tc, base, edge, x, w, gain, bias, offs, out):
         nc.sync.dma_start(windows[0][:], base_blocks[0])
         nc.scalar.dma_start(windows[1][:], base_blocks[1])
 
+        scratch = held.tile([P, 1], F32, name="scratch")
+        nc.vector.memset(scratch[:], 1.0)
+        nc.scalar.activation(scratch[:], scratch[:], ACT.Sqrt)
+
         ident = held.tile([P, P], BF16, name="ident")
         make_identity(nc, ident[:])
         pick = held.tile([n_nodes, n_edges], BF16, name="pick")

@@ -44,7 +44,7 @@ def tile_gnn_s2_kernel(tc, base, edge, x, w, gain, bias, offs, out):
 
         scratch = held.tile([P, 1], F32, name="scratch")
         nc.vector.memset(scratch[:], 1.0)
-        nc.scalar.activation(scratch[:], scratch[:], ACT.Sqrt)
+        nc.scalar.activation(scratch[:], scratch[:], ACT.Abs_reciprocal_sqrt)
 
         ident = held.tile([P, P], BF16, name="ident")
         make_identity(nc, ident[:])
@@ -75,16 +75,15 @@ def tile_gnn_s2_kernel(tc, base, edge, x, w, gain, bias, offs, out):
             mean_var = work.tile([P, 2], F32, name="mean_var")
             nc.vector.bn_aggr(mean_var[:], stats[:])
             rstd = work.tile([P, 1], F32, name="rstd")
-            nc.scalar.activation(rstd[:], mean_var[:, 1:2], ACT.Sqrt, bias=EPS)
-            nc.vector.reciprocal(rstd[:], rstd[:])
+            nc.scalar.activation(rstd[:], mean_var[:, 1:2], ACT.Abs_reciprocal_sqrt, bias=EPS)
 
-            normed = work.tile([P, n_feat], F32, name="normed")
+            centred = work.tile([P, n_feat], F32, name="centred")
             nc.vector.tensor_scalar(
-                normed[:], m_ps[:], mean_var[:, 0:1], rstd[:], ALU.subtract, ALU.mult
+                centred[:], m_ps[:], mean_var[:, 0:1], gain_sb[:, b : b + 1], ALU.subtract, ALU.mult
             )
             h = work.tile([P, n_feat], F32, name="h")
             nc.scalar.activation(
-                h[:], normed[:], ACT.Relu, bias=bias_sb[:, b : b + 1], scale=gain_sb[:, b : b + 1]
+                h[:], centred[:], ACT.Relu, bias=bias_sb[:, b : b + 1], scale=rstd[:]
             )
 
             edge_f32 = work.tile([P, n_feat], F32, name="edge_f32")

@@ -77,13 +77,13 @@ def tile_gnn_s2_kernel(tc, base, edge, x, w, gain, bias, offs, out):
             rstd = work.tile([P, 1], F32, name="rstd")
             nc.scalar.activation(rstd[:], mean_var[:, 1:2], ACT.Abs_reciprocal_sqrt, bias=EPS)
 
-            centred = work.tile([P, n_feat], F32, name="centred")
+            normed = work.tile([P, n_feat], F32, name="normed")
             nc.vector.tensor_scalar(
-                centred[:], m_ps[:], mean_var[:, 0:1], gain_sb[:, b : b + 1], ALU.subtract, ALU.mult
+                normed[:], m_ps[:], mean_var[:, 0:1], rstd[:], ALU.subtract, ALU.mult
             )
             h = work.tile([P, n_feat], F32, name="h")
             nc.scalar.activation(
-                h[:], centred[:], ACT.Relu, bias=bias_sb[:, b : b + 1], scale=rstd[:]
+                h[:], normed[:], ACT.Relu, bias=bias_sb[:, b : b + 1], scale=gain_sb[:, b : b + 1]
             )
 
             edge_f32 = work.tile([P, n_feat], F32, name="edge_f32")

@@ -71,19 +71,20 @@ def tile_gnn_s2_kernel(tc, base, edge, x, w, gain, bias, offs, out):
             nc.tensor.matmul(m_ps[:], edge_t[:], w_sb[:], start=False, stop=True)
 
             stats = work.tile([P, 6], F32, name="stats")
-            nc.vector.bn_stats(stats[:], m_ps[:])
-            mean_var = work.tile([P, 2], F32, name="mean_var")
-            nc.vector.bn_aggr(mean_var[:], stats[:])
+            nc.vector.bn_stats(stats[:], m_ps[:].unsqueeze(2).to_broadcast([P, n_feat, 2]))
+            mean, n_var = stats[:, 1:2], stats[:, 2:3]
             rstd = work.tile([P, 1], F32, name="rstd")
-            nc.scalar.activation(rstd[:], mean_var[:, 1:2], ACT.Abs_reciprocal_sqrt, bias=EPS)
+            nc.scalar.activation(
+                rstd[:], n_var, ACT.Abs_reciprocal_sqrt, bias=EPS, scale=1.0 / n_feat
+            )
 
-            normed = work.tile([P, n_feat], F32, name="normed")
+            centred = work.tile([P, n_feat], F32, name="centred")
             nc.vector.tensor_scalar(
-                normed[:], m_ps[:], mean_var[:, 0:1], rstd[:], ALU.subtract, ALU.mult
+                centred[:], m_ps[:], mean, gain_sb[:, b : b + 1], ALU.subtract, ALU.mult
             )
             h = work.tile([P, n_feat], F32, name="h")
             nc.scalar.activation(
-                h[:], normed[:], ACT.Relu, bias=bias_sb[:, b : b + 1], scale=gain_sb[:, b : b + 1]
+                h[:], centred[:], ACT.Relu, bias=bias_sb[:, b : b + 1], scale=rstd[:]
             )
 
             edge_f32 = work.tile([P, n_feat], F32, name="edge_f32")

@@ -25,12 +25,14 @@ def tile_gnn_s2_kernel(tc, base, edge, x, w, gain, bias, offs, out):
         tc.tile_pool(name="work", bufs=2) as work,
         tc.psum_pool(name="psum", bufs=2) as psum,
     ):
+        edge_blocks = edge.rearrange("(b p) k -> b p k", p=P)
         edge_sb = held.tile([P, n_blocks, n_feat], BF16, name="edge_sb")
-        nc.sync.dma_start(edge_sb[:], edge.rearrange("(b p) k -> p b k", p=P))
-        w_sb = held.tile([n_feat, n_feat], BF16, name="w_sb")
-        nc.scalar.dma_start(w_sb[:], w)
+        nc.sync.dma_start(edge_sb[:, 0, :], edge_blocks[0])
+        nc.scalar.dma_start(edge_sb[:, 1, :], edge_blocks[1])
         x_sb = held.tile([n_nodes, n_feat], BF16, name="x_sb")
         nc.scalar.dma_start(x_sb[:], x)
+        w_sb = held.tile([n_feat, n_feat], BF16, name="w_sb")
+        nc.sync.dma_start(w_sb[:], w)
         offsets = held.tile([P, offs.shape[1]], U16, name="offsets")
         nc.sync.dma_start(offsets[:], offs)
         gain_sb = held.tile([P, n_blocks], F32, name="gain_sb")

@@ -17,15 +17,15 @@ def tile_gnn_s2_kernel(tc, base, edge, x, w, gain, bias, offs, out):
     assert n_edges == n_nodes * n_nodes and n_edges % P == 0 and n_feat == P
     n_blocks = n_edges // P
 
-    base_blocks = base.rearrange("(b p) s -> b p s", p=P)
-    out_blocks = out.rearrange("(b p) s -> b p s", p=P)
+    base_blocks = base.rearrange("(p b) s -> b p s", b=n_blocks)
+    out_blocks = out.rearrange("(p b) s -> b p s", b=n_blocks)
 
     with (
         tc.tile_pool(name="held", bufs=1) as held,
         tc.tile_pool(name="work", bufs=2) as work,
         tc.psum_pool(name="psum", bufs=2) as psum,
     ):
-        edge_blocks = edge.rearrange("(b p) k -> b p k", p=P)
+        edge_blocks = edge.rearrange("(p b) k -> b p k", b=n_blocks)
         edge_sb = held.tile([P, n_blocks, n_feat], BF16, name="edge_sb")
         nc.sync.dma_start(edge_sb[:, 0, :], edge_blocks[0])
         nc.scalar.dma_start(edge_sb[:, 1, :], edge_blocks[1])
@@ -37,9 +37,8 @@ def tile_gnn_s2_kernel(tc, base, edge, x, w, gain, bias, offs, out):
         nc.sync.dma_start(offsets[:], offs)
         gain_sb = held.tile([P, n_blocks], F32, name="gain_sb")
         bias_sb = held.tile([P, n_blocks], F32, name="bias_sb")
-        with nc.allow_non_contiguous_dma(reason="256 single values, one to a partition"):
-            nc.sync.dma_start(gain_sb[:], gain.rearrange("(b p) one -> p (b one)", p=P))
-            nc.scalar.dma_start(bias_sb[:], bias.rearrange("(b p) one -> p (b one)", p=P))
+        nc.sync.dma_start(gain_sb[:], gain.rearrange("(p b) one -> p (b one)", b=n_blocks))
+        nc.scalar.dma_start(bias_sb[:], bias.rearrange("(p b) one -> p (b one)", b=n_blocks))
         windows = [held.tile([P, n_slots], F32, name=f"window{b}") for b in range(n_blocks)]
         nc.sync.dma_start(windows[0][:], base_blocks[0])
         nc.scalar.dma_start(windows[1][:], base_blocks[1])
@@ -50,26 +49,28 @@ def tile_gnn_s2_kernel(tc, base, edge, x, w, gain, bias, offs, out):
 
         ident = held.tile([P, P], BF16, name="ident")
         make_identity(nc, ident[:])
-        pick = held.tile([n_nodes, n_edges], BF16, name="pick")
+        pick = held.tile([n_nodes, n_blocks, P], BF16, name="pick")
         small_ident = ident[0:n_nodes, 0:n_nodes]
-        cube = [n_nodes, n_nodes, n_nodes]
+        per_node = P // n_nodes
+        v_b_a_c = [n_nodes, n_blocks, n_nodes, per_node]
         nc.vector.tensor_tensor(
-            pick[:].rearrange("v (a b) -> v a b", a=n_nodes),
-            small_ident.unsqueeze(2).to_broadcast(cube),
-            small_ident.unsqueeze(1).to_broadcast(cube),
+            pick[:].rearrange("v b (a c) -> v b a c", a=n_nodes),
+            small_ident.unsqueeze(1).unsqueeze(3).to_broadcast(v_b_a_c),
+            small_ident.rearrange("v (c b) -> v b c", b=n_blocks).unsqueeze(2).to_broadcast(v_b_a_c),
             ALU.add,
         )
 
-        for b in range(n_blocks):
-            block = slice(b * P, (b + 1) * P)
+        edge_f32 = held.tile([P, n_blocks, n_feat], F32, name="edge_f32")
+        nc.scalar.copy(edge_f32[:], edge_sb[:])
 
+        for b in range(n_blocks):
             edge_t_ps = psum.tile([n_feat, P], BF16, name="edge_t_ps")
             nc.tensor.transpose(edge_t_ps[:], edge_sb[:, b, :], ident[:])
             edge_t = work.tile([n_feat, P], BF16, name="edge_t")
             nc.vector.tensor_copy(edge_t[:], edge_t_ps[:])
 
             m_ps = psum.tile([P, n_feat], F32, name="m_ps")
-            nc.tensor.matmul(m_ps[:], pick[:, block], x_sb[:], start=True, stop=False)
+            nc.tensor.matmul(m_ps[:], pick[:, b, :], x_sb[:], start=True, stop=False)
             nc.tensor.matmul(m_ps[:], edge_t[:], w_sb[:], start=False, stop=True)
 
             stats = work.tile([P, 6], F32, name="stats")
@@ -89,7 +90,7 @@ def tile_gnn_s2_kernel(tc, base, edge, x, w, gain, bias, offs, out):
                 h[:], centred[:], ACT.Relu, bias=bias_sb[:, b : b + 1], scale=rstd[:]
             )
 
-            edge_f32 = work.tile([P, n_feat], F32, name="edge_f32")
-            nc.scalar.copy(edge_f32[:], edge_sb[:, b, :])
-            nc.vector.tensor_tensor(windows[b][:].indirect(offsets[:]), h[:], edge_f32[:], ALU.add)
+            nc.vector.tensor_tensor(
+                windows[b][:].indirect(offsets[:]), h[:], edge_f32[:, b, :], ALU.add
+            )
             nc.sync.dma_start(out_blocks[b], windows[b][:])

@@ -29,8 +29,9 @@ def tile_gnn_s2_kernel(tc, base, edge, x, w, gain, bias, offs, out):
         edge_sb = held.tile([P, n_blocks, n_feat], BF16, name="edge_sb")
         nc.sync.dma_start(edge_sb[:, 0, :], edge_blocks[0])
         nc.scalar.dma_start(edge_sb[:, 1, :], edge_blocks[1])
-        x_sb = held.tile([n_nodes, n_feat], BF16, name="x_sb")
-        nc.scalar.dma_start(x_sb[:], x)
+        x_sb = held.tile([P, n_feat], BF16, name="x_sb")
+        nc.gpsimd.memset(x_sb[:], 0.0)
+        nc.scalar.dma_start(x_sb[0:n_nodes, :], x)
         w_sb = held.tile([n_feat, n_feat], BF16, name="w_sb")
         nc.sync.dma_start(w_sb[:], w)
         offsets = held.tile([P, offs.shape[1]], U16, name="offsets")
@@ -49,10 +50,10 @@ def tile_gnn_s2_kernel(tc, base, edge, x, w, gain, bias, offs, out):
 
         ident = held.tile([P, P], BF16, name="ident")
         make_identity(nc, ident[:])
-        pick = held.tile([n_nodes, n_blocks, P], BF16, name="pick")
-        small_ident = ident[0:n_nodes, 0:n_nodes]
+        pick = held.tile([P, n_blocks, P], BF16, name="pick")
+        small_ident = ident[:, 0:n_nodes]
         per_node = P // n_nodes
-        v_b_a_c = [n_nodes, n_blocks, n_nodes, per_node]
+        v_b_a_c = [P, n_blocks, n_nodes, per_node]
         nc.vector.tensor_tensor(
             pick[:].rearrange("v b (a c) -> v b a c", a=n_nodes),
             small_ident.unsqueeze(1).unsqueeze(3).to_broadcast(v_b_a_c),

@@ -66,7 +66,7 @@ def tile_gnn_s2_kernel(tc, base, edge, x, w, gain, bias, offs, out):
 
         for b in range(n_blocks):
             edge_t_ps = psum.tile([n_feat, P], BF16, name="edge_t_ps")
-            nc.tensor.transpose(edge_t_ps[:], edge_sb[:, b, :], ident[:])
+            nc.tensor.matmul(edge_t_ps[:], edge_sb[:, b, :], ident[:], start=True, stop=True)
             edge_t = work.tile([n_feat, P], BF16, name="edge_t")
             nc.vector.tensor_copy(edge_t[:], edge_t_ps[:])
 

@@ -31,18 +31,18 @@ def tile_gnn_s2_kernel(tc, base, edge, x, w, gain, bias, offs, out):
         nc.scalar.dma_start(edge_sb[:, 1, :], edge_blocks[1])
         x_sb = held.tile([P, n_feat], BF16, name="x_sb")
         nc.gpsimd.memset(x_sb[:], 0.0)
-        nc.scalar.dma_start(x_sb[0:n_nodes, :], x)
+        nc.sync.dma_start(x_sb[0:n_nodes, :], x)
         w_sb = held.tile([n_feat, n_feat], BF16, name="w_sb")
         nc.sync.dma_start(w_sb[:], w)
-        offsets = held.tile([P, offs.shape[1]], U16, name="offsets")
-        nc.sync.dma_start(offsets[:], offs)
         gain_sb = held.tile([P, n_blocks], F32, name="gain_sb")
         bias_sb = held.tile([P, n_blocks], F32, name="bias_sb")
-        nc.sync.dma_start(gain_sb[:], gain.rearrange("(p b) one -> p (b one)", b=n_blocks))
+        nc.scalar.dma_start(gain_sb[:], gain.rearrange("(p b) one -> p (b one)", b=n_blocks))
         nc.scalar.dma_start(bias_sb[:], bias.rearrange("(p b) one -> p (b one)", b=n_blocks))
         windows = [held.tile([P, n_slots], F32, name=f"window{b}") for b in range(n_blocks)]
         nc.sync.dma_start(windows[0][:], base_blocks[0])
         nc.scalar.dma_start(windows[1][:], base_blocks[1])
+        offsets = held.tile([P, offs.shape[1]], U16, name="offsets")
+        nc.sync.dma_start(offsets[:], offs)
 
         scratch = held.tile([P, 1], F32, name="scratch")
         nc.vector.memset(scratch[:], 1.0)

@@ -30,10 +30,10 @@ def tile_gnn_s2_kernel(tc, base, edge, x, w, gain, bias, offs, out):
         nc.sync.dma_start(edge_sb[:, 0, :], edge_blocks[0])
         nc.scalar.dma_start(edge_sb[:, 1, :], edge_blocks[1])
         x_sb = held.tile([P, n_feat], BF16, name="x_sb")
-        nc.gpsimd.memset(x_sb[:], 0.0)
-        nc.sync.dma_start(x_sb[0:n_nodes, :], x)
+        nc.vector.memset(x_sb[:], 0.0)
         w_sb = held.tile([n_feat, n_feat], BF16, name="w_sb")
         nc.sync.dma_start(w_sb[:], w)
+        nc.sync.dma_start(x_sb[0:n_nodes, :], x)
         gain_sb = held.tile([P, n_blocks], F32, name="gain_sb")
         bias_sb = held.tile([P, n_blocks], F32, name="bias_sb")
         nc.scalar.dma_start(gain_sb[:], gain.rearrange("(p b) one -> p (b one)", b=n_blocks))

@@ -64,6 +64,7 @@ def tile_gnn_s2_kernel(tc, base, edge, x, w, gain, bias, offs, out):
         edge_f32 = held.tile([P, n_blocks, n_feat], F32, name="edge_f32")
         nc.scalar.copy(edge_f32[:], edge_sb[:])
 
+        half = n_feat // 2
         for b in range(n_blocks):
             edge_t_ps = psum.tile([n_feat, P], BF16, name="edge_t_ps")
             nc.tensor.matmul(edge_t_ps[:], edge_sb[:, b, :], ident[:], start=True, stop=True)
@@ -82,14 +83,16 @@ def tile_gnn_s2_kernel(tc, base, edge, x, w, gain, bias, offs, out):
                 rstd[:], n_var, ACT.Abs_reciprocal_sqrt, bias=EPS, scale=1.0 / n_feat
             )
 
-            centred = work.tile([P, n_feat], F32, name="centred")
-            nc.vector.tensor_scalar(
-                centred[:], m_ps[:], mean, gain_sb[:, b : b + 1], ALU.subtract, ALU.mult
-            )
             h = work.tile([P, n_feat], F32, name="h")
-            nc.scalar.activation(
-                h[:], centred[:], ACT.Relu, bias=bias_sb[:, b : b + 1], scale=rstd[:]
-            )
+            for first in range(0, n_feat, half):
+                columns = slice(first, first + half)
+                centred = work.tile([P, half], F32, name=f"centred{first}")
+                nc.vector.tensor_scalar(
+                    centred[:], m_ps[:, columns], mean, gain_sb[:, b : b + 1], ALU.subtract, ALU.mult
+                )
+                nc.scalar.activation(
+                    h[:, columns], centred[:], ACT.Relu, bias=bias_sb[:, b : b + 1], scale=rstd[:]
+                )
 
             nc.vector.tensor_tensor(
                 windows[b][:].indirect(offsets[:]), h[:], edge_f32[:, b, :], ALU.add

@@ -65,11 +65,16 @@ def tile_gnn_s2_kernel(tc, base, edge, x, w, gain, bias, offs, out):
         nc.scalar.copy(edge_f32[:], edge_sb[:])
 
         half = n_feat // 2
+        half_slots = n_slots // 2
         for b in range(n_blocks):
-            edge_t_ps = psum.tile([n_feat, P], BF16, name="edge_t_ps")
-            nc.tensor.matmul(edge_t_ps[:], edge_sb[:, b, :], ident[:], start=True, stop=True)
             edge_t = work.tile([n_feat, P], BF16, name="edge_t")
-            nc.vector.tensor_copy(edge_t[:], edge_t_ps[:])
+            for first in range(0, P, P // 2):
+                edges = slice(first, first + P // 2)
+                edge_t_ps = psum.tile([n_feat, P // 2], BF16, name=f"edge_t_ps{first}")
+                nc.tensor.matmul(
+                    edge_t_ps[:], edge_sb[:, b, :], ident[:, edges], start=True, stop=True
+                )
+                nc.vector.tensor_copy(edge_t[:, edges], edge_t_ps[:])
 
             m_ps = psum.tile([P, n_feat], F32, name="m_ps")
             nc.tensor.matmul(m_ps[:], pick[:, b, :], x_sb[:], start=True, stop=False)
@@ -97,4 +102,6 @@ def tile_gnn_s2_kernel(tc, base, edge, x, w, gain, bias, offs, out):
             nc.vector.tensor_tensor(
                 windows[b][:].indirect(offsets[:]), h[:], edge_f32[:, b, :], ALU.add
             )
-            nc.sync.dma_start(out_blocks[b], windows[b][:])
+            for first in range(0, n_slots, half_slots):
+                slots = slice(first, first + half_slots)
+                nc.sync.dma_start(out_blocks[b][:, slots], windows[b][:, slots])

import concourse.mybir as mybir
from concourse.masks import make_identity

P = 128
EPS = 1e-5
FLOPS = 2 * 256 * 128 * 128

BF16, F32, U16 = mybir.dt.bfloat16, mybir.dt.float32, mybir.dt.uint16
ALU = mybir.AluOpType
ACT = mybir.ActivationFunctionType


def tile_gnn_s2_kernel(tc, base, edge, x, w, gain, bias, offs, out):
    nc = tc.nc
    n_edges, n_slots = base.shape
    n_nodes, n_feat = x.shape
    assert n_edges == n_nodes * n_nodes and n_edges % P == 0 and n_feat == P
    n_blocks = n_edges // P

    base_blocks = base.rearrange("(p b) s -> b p s", b=n_blocks)
    out_blocks = out.rearrange("(p b) s -> b p s", b=n_blocks)

    with (
        tc.tile_pool(name="held", bufs=1) as held,
        tc.tile_pool(name="work", bufs=2) as work,
        tc.psum_pool(name="psum", bufs=2) as psum,
    ):
        edge_blocks = edge.rearrange("(p b) k -> b p k", b=n_blocks)
        edge_sb = held.tile([P, n_blocks, n_feat], BF16, name="edge_sb")
        nc.sync.dma_start(edge_sb[:, 0, :], edge_blocks[0])
        nc.scalar.dma_start(edge_sb[:, 1, :], edge_blocks[1])
        x_sb = held.tile([P, n_feat], BF16, name="x_sb")
        nc.vector.memset(x_sb[:], 0.0)
        w_sb = held.tile([n_feat, n_feat], BF16, name="w_sb")
        nc.sync.dma_start(w_sb[:], w)
        nc.sync.dma_start(x_sb[0:n_nodes, :], x)
        gain_sb = held.tile([P, n_blocks], F32, name="gain_sb")
        bias_sb = held.tile([P, n_blocks], F32, name="bias_sb")
        nc.scalar.dma_start(gain_sb[:], gain.rearrange("(p b) one -> p (b one)", b=n_blocks))
        nc.scalar.dma_start(bias_sb[:], bias.rearrange("(p b) one -> p (b one)", b=n_blocks))
        windows = [held.tile([P, n_slots], F32, name=f"window{b}") for b in range(n_blocks)]
        nc.sync.dma_start(windows[0][:], base_blocks[0])
        nc.scalar.dma_start(windows[1][:], base_blocks[1])
        offsets = held.tile([P, offs.shape[1]], U16, name="offsets")
        nc.sync.dma_start(offsets[:], offs)

        scratch = held.tile([P, 1], F32, name="scratch")
        nc.vector.memset(scratch[:], 1.0)
        nc.scalar.activation(scratch[:], scratch[:], ACT.Abs_reciprocal_sqrt)

        ident = held.tile([P, P], BF16, name="ident")
        make_identity(nc, ident[:])
        pick = held.tile([P, n_blocks, P], BF16, name="pick")
        small_ident = ident[:, 0:n_nodes]
        per_node = P // n_nodes
        v_b_a_c = [P, n_blocks, n_nodes, per_node]
        nc.vector.tensor_tensor(
            pick[:].rearrange("v b (a c) -> v b a c", a=n_nodes),
            small_ident.unsqueeze(1).unsqueeze(3).to_broadcast(v_b_a_c),
            small_ident.rearrange("v (c b) -> v b c", b=n_blocks).unsqueeze(2).to_broadcast(v_b_a_c),
            ALU.add,
        )

        edge_f32 = held.tile([P, n_blocks, n_feat], F32, name="edge_f32")
        nc.scalar.copy(edge_f32[:], edge_sb[:])

        half = n_feat // 2
        half_slots = n_slots // 2
        for b in range(n_blocks):
            edge_t = work.tile([n_feat, P], BF16, name="edge_t")
            for first in range(0, P, P // 2):
                edges = slice(first, first + P // 2)
                edge_t_ps = psum.tile([n_feat, P // 2], BF16, name=f"edge_t_ps{first}")
                nc.tensor.matmul(
                    edge_t_ps[:], edge_sb[:, b, :], ident[:, edges], start=True, stop=True
                )
                nc.vector.tensor_copy(edge_t[:, edges], edge_t_ps[:])

            m_ps = psum.tile([P, n_feat], F32, name="m_ps")
            nc.tensor.matmul(m_ps[:], pick[:, b, :], x_sb[:], start=True, stop=False)
            nc.tensor.matmul(m_ps[:], edge_t[:], w_sb[:], start=False, stop=True)

            stats = work.tile([P, 6], F32, name="stats")
            nc.vector.bn_stats(stats[:], m_ps[:].unsqueeze(2).to_broadcast([P, n_feat, 2]))
            mean, n_var = stats[:, 1:2], stats[:, 2:3]
            rstd = work.tile([P, 1], F32, name="rstd")
            nc.scalar.activation(
                rstd[:], n_var, ACT.Abs_reciprocal_sqrt, bias=EPS, scale=1.0 / n_feat
            )

            h = work.tile([P, n_feat], F32, name="h")
            for first in range(0, n_feat, half):
                columns = slice(first, first + half)
                centred = work.tile([P, half], F32, name=f"centred{first}")
                nc.vector.tensor_scalar(
                    centred[:], m_ps[:, columns], mean, gain_sb[:, b : b + 1], ALU.subtract, ALU.mult
                )
                nc.scalar.activation(
                    h[:, columns], centred[:], ACT.Relu, bias=bias_sb[:, b : b + 1], scale=rstd[:]
                )

            nc.vector.tensor_tensor(
                windows[b][:].indirect(offsets[:]), h[:], edge_f32[:, b, :], ALU.add
            )
            for first in range(0, n_slots, half_slots):
                slots = slice(first, first + half_slots)
                nc.sync.dma_start(out_blocks[b][:, slots], windows[b][:, slots])
